import numpy as np
import ml_dtypes

BF16 = ml_dtypes.bfloat16


def bf(x):
    return np.asarray(x, np.float32).astype(BF16)


def f32(x):
    return np.asarray(x, np.float32)


def f64(x):
    return np.asarray(x).astype(np.float64)


def striped(idx):
    return np.tile(idx.reshape(-1, 16).T, (8, 1))


E, R, K, V, N = 128, 7, 3, 512, 1024


def setup_inputs():
    return {"u": f32(np.random.standard_normal((R * E, V))), "seq_emb": f32(np.random.standard_normal((E, N))), "offs": striped(np.random.permutation(np.tile(np.arange(V), 2))[:N])}


def reference(u, seq_emb, offs):
    idx = offs[:16].T.reshape(-1)
    rad = R // 2
    padded = np.pad(f64(seq_emb), ((0, 0), (rad, rad)))
    ctx = f64(u).reshape(R, E, V)[:, :, idx]
    proj = np.stack([padded[:, i:i + N] for i in range(R)], axis=0) * ctx
    return np.concatenate([proj[m:R - m].max(axis=0) for m in range(K)], axis=0)

@@ -1,0 +1,64 @@
+import concourse.mybir as mybir
+
+FEATURES = 128
+PLACES = 7
+RADIUS = PLACES // 2
+WORDS = 512
+TOKENS = 1024
+PIECE = 512
+PER_COLUMN = 16
+MARGIN = 8
+
+F32 = mybir.dt.float32
+U16 = mybir.dt.uint16
+MULT = mybir.AluOpType.mult
+MAX = mybir.AluOpType.max
+
+
+def tile_multiregionembeddinglayer_kernel(tc, u, seq_emb, offs, out):
+    nc = tc.nc
+    with (
+        tc.tile_pool(name="held", bufs=1) as held,
+        tc.tile_pool(name="products", bufs=2) as products,
+        tc.tile_pool(name="regions", bufs=2) as regions,
+    ):
+        offsets = held.tile([FEATURES, TOKENS // PER_COLUMN], U16, name="offsets")
+        nc.sync.dma_start(offsets[:], offs)
+
+        sequence = held.tile([FEATURES, MARGIN + TOKENS + MARGIN], F32, name="sequence")
+        nc.vector.memset(sequence[:, 0:MARGIN], 0.0)
+        nc.vector.memset(sequence[:, MARGIN + TOKENS :], 0.0)
+        nc.scalar.dma_start(sequence[:, MARGIN : MARGIN + TOKENS], seq_emb)
+
+        by_first_use = sorted(range(PLACES), key=lambda place: abs(place - RADIUS))
+        units = {}
+        for turn, place in enumerate(by_first_use):
+            units[place] = held.tile([FEATURES, WORDS], F32, name=f"unit{place}")
+            queue = nc.sync if turn % 2 == 0 else nc.scalar
+            queue.dma_start(units[place][:], u[place * FEATURES : (place + 1) * FEATURES, :])
+
+        for first in range(0, TOKENS, PIECE):
+            piece_offsets = offsets[:, first // PER_COLUMN : (first + PIECE) // PER_COLUMN]
+
+            def weighted_neighbour(place):
+                product = products.tile([FEATURES, PIECE], F32, name=f"product{place}")
+                shifted = MARGIN + first + place - RADIUS
+                nc.vector.tensor_tensor(
+                    product[:],
+                    units[place][:].indirect(piece_offsets),
+                    sequence[:, shifted : shifted + PIECE],
+                    MULT,
+                )
+                return product
+
+            region = weighted_neighbour(RADIUS)
+            for ring in range(1, RADIUS + 1):
+                before = weighted_neighbour(RADIUS - ring)
+                after = weighted_neighbour(RADIUS + ring)
+                pair = products.tile([FEATURES, PIECE], F32, name="pair")
+                nc.vector.tensor_tensor(pair[:], before[:], after[:], MAX)
+                wider = regions.tile([FEATURES, PIECE], F32, name=f"region{ring}")
+                nc.vector.tensor_tensor(wider[:], region[:], pair[:], MAX)
+                region = wider
+                row = (RADIUS - ring) * FEATURES
+                nc.sync.dma_start(out[row : row + FEATURES, first : first + PIECE], region[:])

@@ -2,7 +2,7 @@ import concourse.mybir as mybir
 
 FEATURES = 128
 PLACES = 7
-RADIUS = PLACES // 2
+MIDDLE = PLACES // 2
 WORDS = 512
 TOKENS = 1024
 PIECE = 512
@@ -17,10 +17,11 @@ MAX = mybir.AluOpType.max
 
 def tile_multiregionembeddinglayer_kernel(tc, u, seq_emb, offs, out):
     nc = tc.nc
+    outwards = sorted(range(PLACES), key=lambda place: abs(place - MIDDLE))
     with (
         tc.tile_pool(name="held", bufs=1) as held,
         tc.tile_pool(name="products", bufs=2) as products,
-        tc.tile_pool(name="regions", bufs=2) as regions,
+        tc.tile_pool(name="maxima", bufs=2) as maxima,
     ):
         offsets = held.tile([FEATURES, TOKENS // PER_COLUMN], U16, name="offsets")
         nc.sync.dma_start(offsets[:], offs)
@@ -30,35 +31,39 @@ def tile_multiregionembeddinglayer_kernel(tc, u, seq_emb, offs, out):
         nc.vector.memset(sequence[:, MARGIN + TOKENS :], 0.0)
         nc.scalar.dma_start(sequence[:, MARGIN : MARGIN + TOKENS], seq_emb)
 
-        by_first_use = sorted(range(PLACES), key=lambda place: abs(place - RADIUS))
         units = {}
-        for turn, place in enumerate(by_first_use):
+        for turn, place in enumerate(outwards):
             units[place] = held.tile([FEATURES, WORDS], F32, name=f"unit{place}")
             queue = nc.sync if turn % 2 == 0 else nc.scalar
             queue.dma_start(units[place][:], u[place * FEATURES : (place + 1) * FEATURES, :])
 
-        for first in range(0, TOKENS, PIECE):
-            piece_offsets = offsets[:, first // PER_COLUMN : (first + PIECE) // PER_COLUMN]
+        def weighted_neighbour(first, place):
+            product = products.tile([FEATURES, PIECE], F32, name=f"product{place}")
+            shifted = MARGIN + first + place - MIDDLE
+            nc.vector.tensor_tensor(
+                product[:],
+                units[place][:].indirect(offsets[:, first // PER_COLUMN : (first + PIECE) // PER_COLUMN]),
+                sequence[:, shifted : shifted + PIECE],
+                MULT,
+            )
+            return product
 
-            def weighted_neighbour(place):
-                product = products.tile([FEATURES, PIECE], F32, name=f"product{place}")
-                shifted = MARGIN + first + place - RADIUS
-                nc.vector.tensor_tensor(
-                    product[:],
-                    units[place][:].indirect(piece_offsets),
-                    sequence[:, shifted : shifted + PIECE],
-                    MULT,
-                )
+        def fold(running, first, place, product):
+            if place == MIDDLE:
                 return product
+            widened = maxima.tile([FEATURES, PIECE], F32, name=f"upto{place}")
+            nc.vector.tensor_tensor(widened[:], running[:], product[:], MAX)
+            if place > MIDDLE:
+                row = (PLACES - 1 - place) * FEATURES
+                nc.sync.dma_start(out[row : row + FEATURES, first : first + PIECE], widened[:])
+            return widened
 
-            region = weighted_neighbour(RADIUS)
-            for ring in range(1, RADIUS + 1):
-                before = weighted_neighbour(RADIUS - ring)
-                after = weighted_neighbour(RADIUS + ring)
-                pair = products.tile([FEATURES, PIECE], F32, name="pair")
-                nc.vector.tensor_tensor(pair[:], before[:], after[:], MAX)
-                wider = regions.tile([FEATURES, PIECE], F32, name=f"region{ring}")
-                nc.vector.tensor_tensor(wider[:], region[:], pair[:], MAX)
-                region = wider
-                row = (RADIUS - ring) * FEATURES
-                nc.sync.dma_start(out[row : row + FEATURES, first : first + PIECE], region[:])
+        running = None
+        ahead = None
+        for first in range(0, TOKENS, PIECE):
+            for place in outwards:
+                product = weighted_neighbour(first, place)
+                if ahead is not None:
+                    running = fold(running, *ahead)
+                ahead = (first, place, product)
+        fold(running, *ahead)

@@ -24,46 +24,39 @@ def tile_multiregionembeddinglayer_kernel(tc, u, seq_emb, offs, out):
         tc.tile_pool(name="maxima", bufs=2) as maxima,
     ):
         offsets = held.tile([FEATURES, TOKENS // PER_COLUMN], U16, name="offsets")
-        nc.sync.dma_start(offsets[:], offs)
-
         sequence = held.tile([FEATURES, MARGIN + TOKENS + MARGIN], F32, name="sequence")
-        nc.vector.memset(sequence[:, 0:MARGIN], 0.0)
-        nc.vector.memset(sequence[:, MARGIN + TOKENS :], 0.0)
-        nc.scalar.dma_start(sequence[:, MARGIN : MARGIN + TOKENS], seq_emb)
+        units = {place: held.tile([FEATURES, WORDS], F32, name=f"unit{place}") for place in outwards}
 
-        units = {}
+        def load_tokens(queue, start, stop):
+            queue.dma_start(sequence[:, MARGIN + start : MARGIN + stop], seq_emb[:, start:stop])
+
+        nc.sync.dma_start(offsets[:], offs)
+        load_tokens(nc.scalar, 0, PIECE + MARGIN)
         for turn, place in enumerate(outwards):
-            units[place] = held.tile([FEATURES, WORDS], F32, name=f"unit{place}")
             queue = nc.sync if turn % 2 == 0 else nc.scalar
             queue.dma_start(units[place][:], u[place * FEATURES : (place + 1) * FEATURES, :])
+        load_tokens(nc.scalar, PIECE + MARGIN, TOKENS)
+        nc.vector.memset(sequence[:, 0:MARGIN], 0.0)
+        nc.vector.memset(sequence[:, MARGIN + TOKENS :], 0.0)
 
-        def weighted_neighbour(first, place):
-            product = products.tile([FEATURES, PIECE], F32, name=f"product{place}")
-            shifted = MARGIN + first + place - MIDDLE
-            nc.vector.tensor_tensor(
-                product[:],
-                units[place][:].indirect(offsets[:, first // PER_COLUMN : (first + PIECE) // PER_COLUMN]),
-                sequence[:, shifted : shifted + PIECE],
-                MULT,
-            )
-            return product
-
-        def fold(running, first, place, product):
-            if place == MIDDLE:
-                return product
-            widened = maxima.tile([FEATURES, PIECE], F32, name=f"upto{place}")
-            nc.vector.tensor_tensor(widened[:], running[:], product[:], MAX)
-            if place > MIDDLE:
-                row = (PLACES - 1 - place) * FEATURES
-                nc.sync.dma_start(out[row : row + FEATURES, first : first + PIECE], widened[:])
-            return widened
-
-        running = None
-        ahead = None
         for first in range(0, TOKENS, PIECE):
+            piece_offsets = offsets[:, first // PER_COLUMN : (first + PIECE) // PER_COLUMN]
+            running = None
             for place in outwards:
-                product = weighted_neighbour(first, place)
-                if ahead is not None:
-                    running = fold(running, *ahead)
-                ahead = (first, place, product)
-        fold(running, *ahead)
+                product = products.tile([FEATURES, PIECE], F32, name=f"product{place}")
+                shifted = MARGIN + first + place - MIDDLE
+                nc.vector.tensor_tensor(
+                    product[:],
+                    units[place][:].indirect(piece_offsets),
+                    sequence[:, shifted : shifted + PIECE],
+                    MULT,
+                )
+                if place == MIDDLE:
+                    running = product
+                    continue
+                widened = maxima.tile([FEATURES, PIECE], F32, name=f"upto{place}")
+                nc.vector.tensor_tensor(widened[:], running[:], product[:], MAX)
+                running = widened
+                if place > MIDDLE:
+                    row = (PLACES - 1 - place) * FEATURES
+                    nc.sync.dma_start(out[row : row + FEATURES, first : first + PIECE], running[:])

@@ -1,4 +1,5 @@
 import concourse.mybir as mybir
+from concourse.masks import make_identity
 
 FEATURES = 128
 PLACES = 7
@@ -8,55 +9,94 @@ TOKENS = 1024
 PIECE = 512
 PER_COLUMN = 16
 MARGIN = 8
+OUTER_RINGS = (1, 0)
 
 F32 = mybir.dt.float32
 U16 = mybir.dt.uint16
 MULT = mybir.AluOpType.mult
 MAX = mybir.AluOpType.max
+RELU = mybir.ActivationFunctionType.Relu
 
 
 def tile_multiregionembeddinglayer_kernel(tc, u, seq_emb, offs, out):
     nc = tc.nc
-    outwards = sorted(range(PLACES), key=lambda place: abs(place - MIDDLE))
+    pieces = range(0, TOKENS, PIECE)
+    inner = [MIDDLE - 1, MIDDLE, MIDDLE + 1]
+    outer = [place for ring in OUTER_RINGS for place in (ring, PLACES - 1 - ring)]
     with (
         tc.tile_pool(name="held", bufs=1) as held,
         tc.tile_pool(name="products", bufs=2) as products,
         tc.tile_pool(name="maxima", bufs=2) as maxima,
+        tc.psum_pool(name="differences", bufs=2) as differences,
+        tc.psum_pool(name="pairs", bufs=2) as pairs,
     ):
         offsets = held.tile([FEATURES, TOKENS // PER_COLUMN], U16, name="offsets")
         sequence = held.tile([FEATURES, MARGIN + TOKENS + MARGIN], F32, name="sequence")
-        units = {place: held.tile([FEATURES, WORDS], F32, name=f"unit{place}") for place in outwards}
+        units = {place: held.tile([FEATURES, WORDS], F32, name=f"unit{place}") for place in outer + inner}
+        plus = held.tile([FEATURES, FEATURES], F32, name="plus")
+        minus = held.tile([FEATURES, FEATURES], F32, name="minus")
 
         def load_tokens(queue, start, stop):
             queue.dma_start(sequence[:, MARGIN + start : MARGIN + stop], seq_emb[:, start:stop])
 
         nc.sync.dma_start(offsets[:], offs)
         load_tokens(nc.scalar, 0, PIECE + MARGIN)
-        for turn, place in enumerate(outwards):
+        for turn, place in enumerate(outer + inner):
             queue = nc.sync if turn % 2 == 0 else nc.scalar
             queue.dma_start(units[place][:], u[place * FEATURES : (place + 1) * FEATURES, :])
-        load_tokens(nc.scalar, PIECE + MARGIN, TOKENS)
+            if turn == 1:
+                load_tokens(nc.scalar, PIECE + MARGIN, TOKENS)
         nc.vector.memset(sequence[:, 0:MARGIN], 0.0)
         nc.vector.memset(sequence[:, MARGIN + TOKENS :], 0.0)
+        make_identity(nc, plus[:])
+        nc.scalar.mul(minus[:], plus[:], -1.0)
 
-        for first in range(0, TOKENS, PIECE):
-            piece_offsets = offsets[:, first // PER_COLUMN : (first + PIECE) // PER_COLUMN]
-            running = None
-            for place in outwards:
-                product = products.tile([FEATURES, PIECE], F32, name=f"product{place}")
-                shifted = MARGIN + first + place - MIDDLE
-                nc.vector.tensor_tensor(
-                    product[:],
-                    units[place][:].indirect(piece_offsets),
-                    sequence[:, shifted : shifted + PIECE],
-                    MULT,
-                )
-                if place == MIDDLE:
-                    running = product
-                    continue
-                widened = maxima.tile([FEATURES, PIECE], F32, name=f"upto{place}")
-                nc.vector.tensor_tensor(widened[:], running[:], product[:], MAX)
-                running = widened
-                if place > MIDDLE:
-                    row = (PLACES - 1 - place) * FEATURES
-                    nc.sync.dma_start(out[row : row + FEATURES, first : first + PIECE], running[:])
+        def look_up(place, first):
+            product = products.tile([FEATURES, PIECE], F32, name=f"product{place}")
+            shifted = MARGIN + first + place - MIDDLE
+            nc.vector.tensor_tensor(
+                product[:],
+                units[place][:].indirect(offsets[:, first // PER_COLUMN : (first + PIECE) // PER_COLUMN]),
+                sequence[:, shifted : shifted + PIECE],
+                MULT,
+            )
+            return product
+
+        def larger_of(a, b, ring):
+            difference = differences.tile([FEATURES, PIECE], F32, name="difference")
+            nc.tensor.matmul(difference[:], plus[:], a[:], start=True, stop=False)
+            nc.tensor.matmul(difference[:], minus[:], b[:], start=False, stop=True)
+            larger = pairs.tile([FEATURES, PIECE], F32, name=f"pair{ring}")
+            nc.tensor.matmul(larger[:], plus[:], b[:], start=True, stop=False)
+            excess = products.tile([FEATURES, PIECE], F32, name="excess")
+            nc.scalar.activation(excess[:], difference[:], RELU)
+            nc.tensor.matmul(larger[:], plus[:], excess[:], start=False, stop=True)
+            return larger
+
+        def widen(running, other, name):
+            widened = maxima.tile([FEATURES, PIECE], F32, name=name)
+            nc.vector.tensor_tensor(widened[:], running[:], other[:], MAX)
+            return widened
+
+        def store(region, first, finished):
+            row = region * FEATURES
+            nc.sync.dma_start(out[row : row + FEATURES, first : first + PIECE], finished[:])
+
+        ring_maxima = {}
+        for first in pieces:
+            for ring in OUTER_RINGS:
+                a = look_up(ring, first)
+                b = look_up(PLACES - 1 - ring, first)
+                if (first, ring) == (pieces[-1], OUTER_RINGS[-1]):
+                    ring_maxima[(ring, first)] = widen(a, b, "pair")
+                else:
+                    ring_maxima[(ring, first)] = larger_of(a, b, ring)
+
+        for first in pieces:
+            running = look_up(inner[0], first)
+            for place in inner[1:]:
+                running = widen(running, look_up(place, first), f"upto{place}")
+            store(MIDDLE - 1, first, running)
+            for ring in OUTER_RINGS:
+                running = widen(running, ring_maxima[(ring, first)], f"region{ring}")
+                store(ring, first, running)

@@ -36,16 +36,18 @@ def tile_multiregionembeddinglayer_kernel(tc, u, seq_emb, offs, out):
         plus = held.tile([FEATURES, FEATURES], F32, name="plus")
         minus = held.tile([FEATURES, FEATURES], F32, name="minus")
 
-        def load_tokens(queue, start, stop):
-            queue.dma_start(sequence[:, MARGIN + start : MARGIN + stop], seq_emb[:, start:stop])
+        def tokens(start, stop):
+            return sequence[:, MARGIN + start : MARGIN + stop], seq_emb[:, start:stop]
+
+        def unit(place):
+            return units[place][:], u[place * FEATURES : (place + 1) * FEATURES, :]
 
         nc.sync.dma_start(offsets[:], offs)
-        load_tokens(nc.scalar, 0, PIECE + MARGIN)
-        for turn, place in enumerate(outer + inner):
-            queue = nc.sync if turn % 2 == 0 else nc.scalar
-            queue.dma_start(units[place][:], u[place * FEATURES : (place + 1) * FEATURES, :])
-            if turn == 1:
-                load_tokens(nc.scalar, PIECE + MARGIN, TOKENS)
+        loads = [tokens(0, PIECE + MARGIN), unit(outer[0]), unit(outer[1]), tokens(PIECE + MARGIN, TOKENS)]
+        loads += [unit(place) for place in outer[2:] + inner]
+        for turn, (tile_side, dram_side) in enumerate(loads):
+            queue = nc.scalar if turn % 2 == 0 else nc.sync
+            queue.dma_start(tile_side, dram_side)
         nc.vector.memset(sequence[:, 0:MARGIN], 0.0)
         nc.vector.memset(sequence[:, MARGIN + TOKENS :], 0.0)
         make_identity(nc, plus[:])
@@ -83,20 +85,24 @@ def tile_multiregionembeddinglayer_kernel(tc, u, seq_emb, offs, out):
             nc.sync.dma_start(out[row : row + FEATURES, first : first + PIECE], finished[:])
 
         ring_maxima = {}
-        for first in pieces:
-            for ring in OUTER_RINGS:
+        for ring in OUTER_RINGS:
+            for first in pieces:
                 a = look_up(ring, first)
                 b = look_up(PLACES - 1 - ring, first)
-                if (first, ring) == (pieces[-1], OUTER_RINGS[-1]):
+                if (ring, first) == (OUTER_RINGS[-1], pieces[-1]):
                     ring_maxima[(ring, first)] = widen(a, b, "pair")
                 else:
                     ring_maxima[(ring, first)] = larger_of(a, b, ring)
 
+        running = {first: look_up(inner[0], first) for first in pieces}
+        for place in inner[1:]:
+            fresh = {first: look_up(place, first) for first in pieces}
+            for first in pieces:
+                running[first] = widen(running[first], fresh[first], f"upto{place}")
         for first in pieces:
-            running = look_up(inner[0], first)
-            for place in inner[1:]:
-                running = widen(running, look_up(place, first), f"upto{place}")
-            store(MIDDLE - 1, first, running)
-            for ring in OUTER_RINGS:
-                running = widen(running, ring_maxima[(ring, first)], f"region{ring}")
-                store(ring, first, running)
+            store(MIDDLE - 1, first, running[first])
+
+        for ring in OUTER_RINGS:
+            for first in pieces:
+                running[first] = widen(running[first], ring_maxima[(ring, first)], f"region{ring}")
+                store(ring, first, running[first])

@@ -9,6 +9,7 @@ TOKENS = 1024
 PIECE = 512
 PER_COLUMN = 16
 MARGIN = 8
+SHARE = 384
 OUTER_RINGS = (1, 0)
 
 F32 = mybir.dt.float32
@@ -64,15 +65,15 @@ def tile_multiregionembeddinglayer_kernel(tc, u, seq_emb, offs, out):
             )
             return product
 
-        def larger_of(a, b, ring):
+        def larger_of(a, b, ring, width=PIECE):
             difference = differences.tile([FEATURES, PIECE], F32, name="difference")
-            nc.tensor.matmul(difference[:], plus[:], a[:], start=True, stop=False)
-            nc.tensor.matmul(difference[:], minus[:], b[:], start=False, stop=True)
+            nc.tensor.matmul(difference[:, :width], plus[:], a[:, :width], start=True, stop=False)
+            nc.tensor.matmul(difference[:, :width], minus[:], b[:, :width], start=False, stop=True)
             larger = pairs.tile([FEATURES, PIECE], F32, name=f"pair{ring}")
-            nc.tensor.matmul(larger[:], plus[:], b[:], start=True, stop=False)
+            nc.tensor.matmul(larger[:, :width], plus[:], b[:, :width], start=True, stop=False)
             excess = products.tile([FEATURES, PIECE], F32, name="excess")
-            nc.scalar.activation(excess[:], difference[:], RELU)
-            nc.tensor.matmul(larger[:], plus[:], excess[:], start=False, stop=True)
+            nc.scalar.activation(excess[:, :width], difference[:, :width], RELU)
+            nc.tensor.matmul(larger[:, :width], plus[:], excess[:, :width], start=False, stop=True)
             return larger
 
         def widen(running, other, name):
@@ -90,7 +91,9 @@ def tile_multiregionembeddinglayer_kernel(tc, u, seq_emb, offs, out):
                 a = look_up(ring, first)
                 b = look_up(PLACES - 1 - ring, first)
                 if (ring, first) == (OUTER_RINGS[-1], pieces[-1]):
-                    ring_maxima[(ring, first)] = widen(a, b, "pair")
+                    ring_maxima[(ring, first)] = larger_of(a, b, ring, width=SHARE)
+                    rest = maxima.tile([FEATURES, PIECE], F32, name="rest")
+                    nc.vector.tensor_tensor(rest[:, SHARE:], a[:, SHARE:], b[:, SHARE:], MAX)
                 else:
                     ring_maxima[(ring, first)] = larger_of(a, b, ring)
 
@@ -104,5 +107,13 @@ def tile_multiregionembeddinglayer_kernel(tc, u, seq_emb, offs, out):
 
         for ring in OUTER_RINGS:
             for first in pieces:
-                running[first] = widen(running[first], ring_maxima[(ring, first)], f"region{ring}")
+                if (ring, first) == (OUTER_RINGS[-1], pieces[-1]):
+                    widened = maxima.tile([FEATURES, PIECE], F32, name=f"region{ring}")
+                    nc.vector.tensor_tensor(widened[:, SHARE:], running[first][:, SHARE:], rest[:, SHARE:], MAX)
+                    nc.vector.tensor_tensor(
+                        widened[:, :SHARE], running[first][:, :SHARE], ring_maxima[(ring, first)][:, :SHARE], MAX
+                    )
+                    running[first] = widened
+                else:
+                    running[first] = widen(running[first], ring_maxima[(ring, first)], f"region{ring}")
                 store(ring, first, running[first])

import concourse.mybir as mybir
from concourse.masks import make_identity

FEATURES = 128
PLACES = 7
MIDDLE = PLACES // 2
WORDS = 512
TOKENS = 1024
PIECE = 512
PER_COLUMN = 16
MARGIN = 8
SHARE = 384
OUTER_RINGS = (1, 0)

F32 = mybir.dt.float32
U16 = mybir.dt.uint16
MULT = mybir.AluOpType.mult
MAX = mybir.AluOpType.max
RELU = mybir.ActivationFunctionType.Relu


def tile_multiregionembeddinglayer_kernel(tc, u, seq_emb, offs, out):
    nc = tc.nc
    pieces = range(0, TOKENS, PIECE)
    inner = [MIDDLE - 1, MIDDLE, MIDDLE + 1]
    outer = [place for ring in OUTER_RINGS for place in (ring, PLACES - 1 - ring)]
    with (
        tc.tile_pool(name="held", bufs=1) as held,
        tc.tile_pool(name="products", bufs=2) as products,
        tc.tile_pool(name="maxima", bufs=2) as maxima,
        tc.psum_pool(name="differences", bufs=2) as differences,
        tc.psum_pool(name="pairs", bufs=2) as pairs,
    ):
        offsets = held.tile([FEATURES, TOKENS // PER_COLUMN], U16, name="offsets")
        sequence = held.tile([FEATURES, MARGIN + TOKENS + MARGIN], F32, name="sequence")
        units = {place: held.tile([FEATURES, WORDS], F32, name=f"unit{place}") for place in outer + inner}
        plus = held.tile([FEATURES, FEATURES], F32, name="plus")
        minus = held.tile([FEATURES, FEATURES], F32, name="minus")

        def tokens(start, stop):
            return sequence[:, MARGIN + start : MARGIN + stop], seq_emb[:, start:stop]

        def unit(place):
            return units[place][:], u[place * FEATURES : (place + 1) * FEATURES, :]

        nc.sync.dma_start(offsets[:], offs)
        loads = [tokens(0, PIECE + MARGIN), unit(outer[0]), unit(outer[1]), tokens(PIECE + MARGIN, TOKENS)]
        loads += [unit(place) for place in outer[2:] + inner]
        for turn, (tile_side, dram_side) in enumerate(loads):
            queue = nc.scalar if turn % 2 == 0 else nc.sync
            queue.dma_start(tile_side, dram_side)
        nc.vector.memset(sequence[:, 0:MARGIN], 0.0)
        nc.vector.memset(sequence[:, MARGIN + TOKENS :], 0.0)
        make_identity(nc, plus[:])
        nc.scalar.mul(minus[:], plus[:], -1.0)

        def look_up(place, first):
            product = products.tile([FEATURES, PIECE], F32, name=f"product{place}")
            shifted = MARGIN + first + place - MIDDLE
            nc.vector.tensor_tensor(
                product[:],
                units[place][:].indirect(offsets[:, first // PER_COLUMN : (first + PIECE) // PER_COLUMN]),
                sequence[:, shifted : shifted + PIECE],
                MULT,
            )
            return product

        def larger_of(a, b, ring, width=PIECE):
            difference = differences.tile([FEATURES, PIECE], F32, name="difference")
            nc.tensor.matmul(difference[:, :width], plus[:], a[:, :width], start=True, stop=False)
            nc.tensor.matmul(difference[:, :width], minus[:], b[:, :width], start=False, stop=True)
            larger = pairs.tile([FEATURES, PIECE], F32, name=f"pair{ring}")
            nc.tensor.matmul(larger[:, :width], plus[:], b[:, :width], start=True, stop=False)
            excess = products.tile([FEATURES, PIECE], F32, name="excess")
            nc.scalar.activation(excess[:, :width], difference[:, :width], RELU)
            nc.tensor.matmul(larger[:, :width], plus[:], excess[:, :width], start=False, stop=True)
            return larger

        def widen(running, other, name):
            widened = maxima.tile([FEATURES, PIECE], F32, name=name)
            nc.vector.tensor_tensor(widened[:], running[:], other[:], MAX)
            return widened

        def store(region, first, finished):
            row = region * FEATURES
            nc.sync.dma_start(out[row : row + FEATURES, first : first + PIECE], finished[:])

        ring_maxima = {}
        for ring in OUTER_RINGS:
            for first in pieces:
                a = look_up(ring, first)
                b = look_up(PLACES - 1 - ring, first)
                if (ring, first) == (OUTER_RINGS[-1], pieces[-1]):
                    ring_maxima[(ring, first)] = larger_of(a, b, ring, width=SHARE)
                    rest = maxima.tile([FEATURES, PIECE], F32, name="rest")
                    nc.vector.tensor_tensor(rest[:, SHARE:], a[:, SHARE:], b[:, SHARE:], MAX)
                else:
                    ring_maxima[(ring, first)] = larger_of(a, b, ring)

        running = {first: look_up(inner[0], first) for first in pieces}
        for place in inner[1:]:
            fresh = {first: look_up(place, first) for first in pieces}
            for first in pieces:
                running[first] = widen(running[first], fresh[first], f"upto{place}")
        for first in pieces:
            store(MIDDLE - 1, first, running[first])

        for ring in OUTER_RINGS:
            for first in pieces:
                if (ring, first) == (OUTER_RINGS[-1], pieces[-1]):
                    widened = maxima.tile([FEATURES, PIECE], F32, name=f"region{ring}")
                    nc.vector.tensor_tensor(widened[:, SHARE:], running[first][:, SHARE:], rest[:, SHARE:], MAX)
                    nc.vector.tensor_tensor(
                        widened[:, :SHARE], running[first][:, :SHARE], ring_maxima[(ring, first)][:, :SHARE], MAX
                    )
                    running[first] = widened
                else:
                    running[first] = widen(running[first], ring_maxima[(ring, first)], f"region{ring}")
                store(ring, first, running[first])
